import numpy as np
import ml_dtypes

BF16 = ml_dtypes.bfloat16


def bf(x):
    return np.asarray(x, np.float32).astype(BF16)


def f32(x):
    return np.asarray(x, np.float32)


def f64(x):
    return np.asarray(x).astype(np.float64)


def striped(idx):
    return np.tile(idx.reshape(-1, 16).T, (8, 1))


C, S, N, T, R, M, O = 128, 1024, 2048, 8, 16, 256, 256


def setup_inputs():
    return {"table": bf(np.random.standard_normal((C, S))), "w": bf(np.random.standard_normal((C, M)) / np.sqrt(C)), "u": bf(np.random.standard_normal((M, O)) * T / np.sqrt(M)), "b": f32(0.2 * np.random.standard_normal((O, 1))), "offs": striped(np.random.permutation(np.tile(np.arange(S), 2))[:N])}


def reference(table, w, u, b, offs):
    idx = offs[:16].T.reshape(-1)
    h = f64(w).T @ f64(table)[:, idx]
    return f64(u).T @ h / T + 2.0 * f64(b)

@@ -1,0 +1,99 @@
+import concourse.mybir as mybir
+
+BF16 = mybir.dt.bfloat16
+F32 = mybir.dt.float32
+U16 = mybir.dt.uint16
+
+P = 128
+S = 1024
+N = 2048
+M = 256
+O = 256
+TERMS = 8
+
+PIECE = 512
+LAST_PIECE = N - PIECE
+STRIP = 256
+M_BLOCKS = M // P
+O_BLOCKS = O // P
+PSUM_BANKS = 8
+WARM_MATMULS = 3
+
+FLOPS = 2 * P * M * N + 2 * M * O * N
+
+
+def tile_skconv2d_kernel(tc, table, w, u, b, offs, out):
+    nc = tc.nc
+    mult, add = mybir.AluOpType.mult, mybir.AluOpType.add
+    identity = mybir.ActivationFunctionType.Identity
+
+    with (
+        tc.tile_pool(name="held", bufs=1) as held,
+        tc.psum_pool(name="banks", bufs=PSUM_BANKS) as banks,
+    ):
+        zeros = held.tile([P, PIECE], BF16, name="zeros")
+        nc.vector.memset(zeros[:], 0.0)
+        warm_ps = banks.tile([P, PIECE], F32, name="warm_ps", tag="bank")
+        for repeat in range(WARM_MATMULS):
+            nc.tensor.matmul(warm_ps[:], zeros[:, 0:P], zeros[:], start=True, stop=True)
+
+        offsets = held.tile([P, N // 16], U16, name="offsets")
+        nc.sync.dma_start(offsets[:], offs)
+        table_sb = held.tile([P, S], BF16, name="table_sb")
+        nc.sync.dma_start(table_sb[:], table)
+        w_sb = held.tile([P, M], BF16, name="w_sb")
+        nc.scalar.dma_start(w_sb[:], w)
+        u_sb = held.tile([P, M_BLOCKS, O], BF16, name="u_sb")
+        nc.scalar.dma_start(u_sb[:], u.rearrange("(mb k) o -> k mb o", k=P))
+        twice_b = []
+        for ob in range(O_BLOCKS):
+            b_sb = held.tile([P, 1], F32, name=f"b_sb{ob}")
+            nc.scalar.dma_start(b_sb[:], b[ob * P : (ob + 1) * P, :])
+            doubled = held.tile([P, 1], F32, name=f"twice_b{ob}")
+            nc.vector.tensor_scalar_mul(doubled[:], b_sb[:], 2.0)
+            twice_b.append(doubled)
+
+        h_sb = [held.tile([P, N], BF16, name=f"h_sb{mb}") for mb in range(M_BLOCKS)]
+        out_sb = [held.tile([P, N], F32, name=f"out_sb{ob}") for ob in range(O_BLOCKS)]
+
+        def down_project(first, width):
+            columns = slice(first, first + width)
+            picked = table_sb[:].indirect(offsets[:, first // 16 : (first + width) // 16])
+            for mb in range(M_BLOCKS):
+                h_ps = banks.tile([P, width], F32, name="h_ps", tag="bank")
+                nc.tensor.matmul(h_ps[:], w_sb[:, mb * P : (mb + 1) * P], picked, start=True, stop=True)
+                if mb == 0:
+                    nc.scalar.copy(h_sb[mb][:, columns], h_ps[:])
+                else:
+                    nc.vector.tensor_copy(h_sb[mb][:, columns], h_ps[:])
+
+        def up_project(first, width, scalar_tiles_queue):
+            columns = slice(first, first + width)
+            for ob in range(O_BLOCKS):
+                out_ps = banks.tile([P, width], F32, name="out_ps", tag="bank")
+                for strip in range(0, width, STRIP):
+                    for mb in range(M_BLOCKS):
+                        nc.tensor.matmul(
+                            out_ps[:, strip : strip + STRIP],
+                            u_sb[:, mb, ob * P : (ob + 1) * P],
+                            h_sb[mb][:, first + strip : first + strip + STRIP],
+                            start=(mb == 0),
+                            stop=(mb == M_BLOCKS - 1),
+                        )
+                if ob == 0:
+                    nc.scalar.activation(
+                        out_sb[ob][:, columns], out_ps[:], identity, bias=twice_b[ob][:], scale=1.0 / TERMS
+                    )
+                    scalar_tiles_queue.dma_start(out[ob * P : (ob + 1) * P, columns], out_sb[ob][:, columns])
+                else:
+                    nc.vector.tensor_scalar(out_sb[ob][:, columns], out_ps[:], 1.0 / TERMS, twice_b[ob][:], mult, add)
+                    nc.sync.dma_start(out[ob * P : (ob + 1) * P, columns], out_sb[ob][:, columns])
+
+        for first in range(0, LAST_PIECE, PIECE):
+            down_project(first, PIECE)
+        for first in range(0, LAST_PIECE, PIECE):
+            up_project(first, PIECE, nc.scalar)
+        for first in range(LAST_PIECE, N, STRIP):
+            down_project(first, STRIP)
+        for first in range(LAST_PIECE, N, STRIP):
+            up_project(first, STRIP, nc.sync)

@@ -17,7 +17,6 @@ STRIP = 256
 M_BLOCKS = M // P
 O_BLOCKS = O // P
 PSUM_BANKS = 8
-WARM_MATMULS = 3
 
 FLOPS = 2 * P * M * N + 2 * M * O * N
 
@@ -31,18 +30,12 @@ def tile_skconv2d_kernel(tc, table, w, u, b, offs, out):
         tc.tile_pool(name="held", bufs=1) as held,
         tc.psum_pool(name="banks", bufs=PSUM_BANKS) as banks,
     ):
-        zeros = held.tile([P, PIECE], BF16, name="zeros")
-        nc.vector.memset(zeros[:], 0.0)
-        warm_ps = banks.tile([P, PIECE], F32, name="warm_ps", tag="bank")
-        for repeat in range(WARM_MATMULS):
-            nc.tensor.matmul(warm_ps[:], zeros[:, 0:P], zeros[:], start=True, stop=True)
-
         offsets = held.tile([P, N // 16], U16, name="offsets")
         nc.sync.dma_start(offsets[:], offs)
-        table_sb = held.tile([P, S], BF16, name="table_sb")
-        nc.sync.dma_start(table_sb[:], table)
         w_sb = held.tile([P, M], BF16, name="w_sb")
-        nc.scalar.dma_start(w_sb[:], w)
+        nc.sync.dma_start(w_sb[:], w)
+        table_sb = held.tile([P, S], BF16, name="table_sb")
+        nc.scalar.dma_start(table_sb[:], table)
         u_sb = held.tile([P, M_BLOCKS, O], BF16, name="u_sb")
         nc.scalar.dma_start(u_sb[:], u.rearrange("(mb k) o -> k mb o", k=P))
         twice_b = []

@@ -85,7 +85,7 @@ def tile_skconv2d_kernel(tc, table, w, u, b, offs, out):
         for first in range(0, LAST_PIECE, PIECE):
             down_project(first, PIECE)
         for first in range(0, LAST_PIECE, PIECE):
-            up_project(first, PIECE, nc.scalar)
+            up_project(first, PIECE, nc.scalar if first + PIECE < LAST_PIECE else nc.sync)
         for first in range(LAST_PIECE, N, STRIP):
             down_project(first, STRIP)
         for first in range(LAST_PIECE, N, STRIP):

@@ -60,33 +60,46 @@ def tile_skconv2d_kernel(tc, table, w, u, b, offs, out):
                 else:
                     nc.vector.tensor_copy(h_sb[mb][:, columns], h_ps[:])
 
-        def up_project(first, width, scalar_tiles_queue):
-            columns = slice(first, first + width)
-            for ob in range(O_BLOCKS):
-                out_ps = banks.tile([P, width], F32, name="out_ps", tag="bank")
-                for strip in range(0, width, STRIP):
-                    for mb in range(M_BLOCKS):
-                        nc.tensor.matmul(
-                            out_ps[:, strip : strip + STRIP],
-                            u_sb[:, mb, ob * P : (ob + 1) * P],
-                            h_sb[mb][:, first + strip : first + strip + STRIP],
-                            start=(mb == 0),
-                            stop=(mb == M_BLOCKS - 1),
-                        )
-                if ob == 0:
-                    nc.scalar.activation(
-                        out_sb[ob][:, columns], out_ps[:], identity, bias=twice_b[ob][:], scale=1.0 / TERMS
+        def up_sum(ob, columns):
+            width = columns.stop - columns.start
+            out_ps = banks.tile([P, width], F32, name="out_ps", tag="bank")
+            for strip in range(0, width, STRIP):
+                strip_width = min(STRIP, width)
+                for mb in range(M_BLOCKS):
+                    nc.tensor.matmul(
+                        out_ps[:, strip : strip + strip_width],
+                        u_sb[:, mb, ob * P : (ob + 1) * P],
+                        h_sb[mb][:, columns.start + strip : columns.start + strip + strip_width],
+                        start=(mb == 0),
+                        stop=(mb == M_BLOCKS - 1),
                     )
-                    scalar_tiles_queue.dma_start(out[ob * P : (ob + 1) * P, columns], out_sb[ob][:, columns])
-                else:
-                    nc.vector.tensor_scalar(out_sb[ob][:, columns], out_ps[:], 1.0 / TERMS, twice_b[ob][:], mult, add)
-                    nc.sync.dma_start(out[ob * P : (ob + 1) * P, columns], out_sb[ob][:, columns])
+            return out_ps
+
+        def finish_on_scalar(ob, columns, out_ps):
+            nc.scalar.activation(
+                out_sb[ob][:, columns], out_ps[:], identity, bias=twice_b[ob][:], scale=1.0 / TERMS
+            )
+
+        def finish_on_vector(ob, columns, out_ps):
+            nc.vector.tensor_scalar(out_sb[ob][:, columns], out_ps[:], 1.0 / TERMS, twice_b[ob][:], mult, add)
+
+        def store(queue, ob, columns):
+            queue.dma_start(out[ob * P : (ob + 1) * P, columns], out_sb[ob][:, columns])
 
         for first in range(0, LAST_PIECE, PIECE):
             down_project(first, PIECE)
         for first in range(0, LAST_PIECE, PIECE):
-            up_project(first, PIECE, nc.scalar if first + PIECE < LAST_PIECE else nc.sync)
+            columns = slice(first, first + PIECE)
+            finish_on_scalar(0, columns, up_sum(0, columns))
+            store(nc.scalar if first + PIECE < LAST_PIECE else nc.sync, 0, columns)
+            finish_on_vector(1, columns, up_sum(1, columns))
+            store(nc.sync, 1, columns)
         for first in range(LAST_PIECE, N, STRIP):
             down_project(first, STRIP)
         for first in range(LAST_PIECE, N, STRIP):
-            up_project(first, STRIP, nc.sync)
+            middle, end = first + STRIP // 2, first + STRIP
+            for ob in range(O_BLOCKS):
+                left, right = slice(first, middle), slice(middle, end)
+                finish_on_vector(ob, left, up_sum(ob, left))
+                finish_on_scalar(ob, right, up_sum(ob, right))
+                store(nc.sync, ob, slice(first, end))

import concourse.mybir as mybir

BF16 = mybir.dt.bfloat16
F32 = mybir.dt.float32
U16 = mybir.dt.uint16

P = 128
S = 1024
N = 2048
M = 256
O = 256
TERMS = 8

PIECE = 512
LAST_PIECE = N - PIECE
STRIP = 256
M_BLOCKS = M // P
O_BLOCKS = O // P
PSUM_BANKS = 8

FLOPS = 2 * P * M * N + 2 * M * O * N


def tile_skconv2d_kernel(tc, table, w, u, b, offs, out):
    nc = tc.nc
    mult, add = mybir.AluOpType.mult, mybir.AluOpType.add
    identity = mybir.ActivationFunctionType.Identity

    with (
        tc.tile_pool(name="held", bufs=1) as held,
        tc.psum_pool(name="banks", bufs=PSUM_BANKS) as banks,
    ):
        offsets = held.tile([P, N // 16], U16, name="offsets")
        nc.sync.dma_start(offsets[:], offs)
        w_sb = held.tile([P, M], BF16, name="w_sb")
        nc.sync.dma_start(w_sb[:], w)
        table_sb = held.tile([P, S], BF16, name="table_sb")
        nc.scalar.dma_start(table_sb[:], table)
        u_sb = held.tile([P, M_BLOCKS, O], BF16, name="u_sb")
        nc.scalar.dma_start(u_sb[:], u.rearrange("(mb k) o -> k mb o", k=P))
        twice_b = []
        for ob in range(O_BLOCKS):
            b_sb = held.tile([P, 1], F32, name=f"b_sb{ob}")
            nc.scalar.dma_start(b_sb[:], b[ob * P : (ob + 1) * P, :])
            doubled = held.tile([P, 1], F32, name=f"twice_b{ob}")
            nc.vector.tensor_scalar_mul(doubled[:], b_sb[:], 2.0)
            twice_b.append(doubled)

        h_sb = [held.tile([P, N], BF16, name=f"h_sb{mb}") for mb in range(M_BLOCKS)]
        out_sb = [held.tile([P, N], F32, name=f"out_sb{ob}") for ob in range(O_BLOCKS)]

        def down_project(first, width):
            columns = slice(first, first + width)
            picked = table_sb[:].indirect(offsets[:, first // 16 : (first + width) // 16])
            for mb in range(M_BLOCKS):
                h_ps = banks.tile([P, width], F32, name="h_ps", tag="bank")
                nc.tensor.matmul(h_ps[:], w_sb[:, mb * P : (mb + 1) * P], picked, start=True, stop=True)
                if mb == 0:
                    nc.scalar.copy(h_sb[mb][:, columns], h_ps[:])
                else:
                    nc.vector.tensor_copy(h_sb[mb][:, columns], h_ps[:])

        def up_sum(ob, columns):
            width = columns.stop - columns.start
            out_ps = banks.tile([P, width], F32, name="out_ps", tag="bank")
            for strip in range(0, width, STRIP):
                strip_width = min(STRIP, width)
                for mb in range(M_BLOCKS):
                    nc.tensor.matmul(
                        out_ps[:, strip : strip + strip_width],
                        u_sb[:, mb, ob * P : (ob + 1) * P],
                        h_sb[mb][:, columns.start + strip : columns.start + strip + strip_width],
                        start=(mb == 0),
                        stop=(mb == M_BLOCKS - 1),
                    )
            return out_ps

        def finish_on_scalar(ob, columns, out_ps):
            nc.scalar.activation(
                out_sb[ob][:, columns], out_ps[:], identity, bias=twice_b[ob][:], scale=1.0 / TERMS
            )

        def finish_on_vector(ob, columns, out_ps):
            nc.vector.tensor_scalar(out_sb[ob][:, columns], out_ps[:], 1.0 / TERMS, twice_b[ob][:], mult, add)

        def store(queue, ob, columns):
            queue.dma_start(out[ob * P : (ob + 1) * P, columns], out_sb[ob][:, columns])

        for first in range(0, LAST_PIECE, PIECE):
            down_project(first, PIECE)
        for first in range(0, LAST_PIECE, PIECE):
            columns = slice(first, first + PIECE)
            finish_on_scalar(0, columns, up_sum(0, columns))
            store(nc.scalar if first + PIECE < LAST_PIECE else nc.sync, 0, columns)
            finish_on_vector(1, columns, up_sum(1, columns))
            store(nc.sync, 1, columns)
        for first in range(LAST_PIECE, N, STRIP):
            down_project(first, STRIP)
        for first in range(LAST_PIECE, N, STRIP):
            middle, end = first + STRIP // 2, first + STRIP
            for ob in range(O_BLOCKS):
                left, right = slice(first, middle), slice(middle, end)
                finish_on_vector(ob, left, up_sum(ob, left))
                finish_on_scalar(ob, right, up_sum(ob, right))
                store(nc.sync, ob, slice(first, end))
